import numpy as np
import ml_dtypes


def mxq(x, axis, fmt="e4m3"):
    dtype, down = {"e4m3": (ml_dtypes.float8_e4m3fn, 7), "e5m2": (ml_dtypes.float8_e5m2, 14)}[fmt]
    v = np.moveaxis(np.asarray(x, np.float32).astype(ml_dtypes.bfloat16).astype(np.float64), axis, -1)
    blocks = v.reshape(v.shape[:-1] + (-1, 32))
    amax = np.abs(blocks).max(-1, keepdims=True)
    byte = np.maximum(np.where(amax > 0, np.frexp(amax)[1] - 1 + 127, 0) - down, 1)
    scale = np.exp2(byte - 127.0)
    codes = (blocks / scale).astype(np.float32).astype(dtype).astype(np.float64)
    return np.moveaxis((codes * scale).reshape(v.shape), -1, axis)


WIDE = False


def mx_kscale(k):
    if not WIDE:
        return np.ones(k)
    levels = np.array([10, -10, 5, -5, 0])
    a = np.random.permutation(np.resize(levels, k // 512 * 4)).reshape(k // 512, 4)
    idx = np.arange(k)
    return np.exp2(a[idx // 512, idx % 128 // 32])


BF16 = ml_dtypes.bfloat16


def bf(x):
    return np.asarray(x, np.float32).astype(BF16)


def f64(x):
    return np.asarray(x).astype(np.float64)


B, N, L, H, S, R, C = 2, 512, 12, 64, 2, 2, 512
M = R * S * H
BN_EPS = 1e-5


def setup_inputs():
    s = mx_kscale(L * M).reshape(L, M)
    t = mx_kscale(C)
    return {"hops": bf((1.7 * np.random.standard_normal((B, N, L, M)) + 0.4 * np.random.standard_normal((L, M))) * s),
            "weight": bf(np.random.standard_normal((L, M, C)) * 0.6 / np.sqrt(L * M) / s[:, :, None]),
            "gamma": bf((1.0 + 0.1 * np.random.standard_normal(C)) * t),
            "beta": bf(0.2 * np.random.standard_normal(C) * t),
            "w2": bf(np.random.standard_normal((C, C)) / np.sqrt(C) / t[None, :]),
            "b2": bf(0.2 * np.random.standard_normal(C))}


def reference(hops, weight, gamma, beta, w2, b2):
    hf = f64(hops).reshape(B * N, L * M)
    wm = f64(weight).reshape(L * M, C)
    flat = mxq(hf, 1, "e4m3") @ mxq(wm, 0, "e4m3")
    mean = flat.mean(axis=0)
    var = flat.var(axis=0)
    normed = (flat - mean) * (1.0 / np.sqrt(var + BN_EPS)) * f64(gamma) + f64(beta)
    y = np.maximum(normed, 0.0)
    out = (mxq(y, 1, "e4m3") @ mxq(f64(w2), 1, "e4m3").T) + f64(b2)
    return out.reshape(B, N, C)

@@ -1,0 +1,331 @@
+from contextlib import ExitStack
+
+import concourse.mybir as mybir
+from concourse.masks import make_identity
+
+F32 = mybir.dt.float32
+BF16 = mybir.dt.bfloat16
+U32 = mybir.dt.uint32
+U8 = mybir.dt.uint8
+FP8X4 = mybir.dt.float8_e4m3fn_x4
+ACT = mybir.ActivationFunctionType
+ALU = mybir.AluOpType
+
+P = 128
+ROWS = 1024
+K1 = 3072
+C = 512
+PASSES = K1 // 512
+EPS = 1e-5
+FLOPS = 2 * ROWS * K1 * C + 2 * ROWS * C * C
+
+
+def tile_ginconvfft_pb_kernel(tc, hops, weight, gamma, beta, w2, b2, out):
+    nc = tc.nc
+    hf = hops.rearrange("b n l m -> (b n) (l m)")
+    wm = weight.rearrange("l m c -> (l m) c")
+    of = out.rearrange("b n c -> (b n) c")
+
+    with ExitStack() as ctx:
+        keep = ctx.enter_context(tc.tile_pool(name="keep", bufs=1))
+        ring = ctx.enter_context(tc.tile_pool(name="ring", bufs=2))
+        psum = ctx.enter_context(tc.psum_pool(name="psum", bufs=1))
+        ctx.enter_context(tc.manual_schedule())
+
+        eps = keep.tile([P, 1], F32, name="eps")
+        warm = keep.tile([P, 1], F32, name="warm")
+        ident_f = keep.tile([P, P], F32, name="ident_f")
+        ident_b = keep.tile([P, P], BF16, name="ident_b")
+        ones = keep.tile([P, P], BF16, name="ones")
+        gb = keep.tile([P, P], BF16, name="gb")
+        bz = keep.tile([P, C], BF16, name="bz")
+        hraw = [keep.tile([P, K1], BF16, name="hraw%d" % i) for i in range(8)]
+        w2raw = keep.tile([P, 4 * C], BF16, name="w2raw")
+        wraw = [keep.tile([P, 4 * C], BF16, name="wraw%d" % g) for g in range(PASSES)]
+        wg = [keep.tile([P, 4 * C], BF16, name="wg%d" % g, align_bytes=64) for g in range(PASSES)]
+        hc = keep.tile([P, PASSES * ROWS], U32, name="hc", align_bytes=64)
+        hs = keep.tile([P, PASSES * ROWS], U8, name="hs", align_bytes=64)
+        wc = keep.tile([P, PASSES * C], U32, name="wc", align_bytes=64)
+        ws = keep.tile([P, PASSES * C], U8, name="ws", align_bytes=64)
+        w2g = keep.tile([P, 4 * C], BF16, name="w2g", align_bytes=64)
+        w2c = keep.tile([P, C], U32, name="w2c", align_bytes=64)
+        w2s = keep.tile([P, C], U8, name="w2s", align_bytes=64)
+        yp = keep.tile([P, 4 * ROWS], BF16, name="yp")
+        yg = keep.tile([P, 4 * ROWS], BF16, name="yg", align_bytes=64)
+        yc = keep.tile([P, ROWS], U32, name="yc", align_bytes=64)
+        ys = keep.tile([P, ROWS], U8, name="ys", align_bytes=64)
+        b2bc = keep.tile([P, C], F32, name="b2bc")
+        gbf = keep.tile([P, 8], F32, name="gbf")
+
+        nc.sync.dma_start(
+            out=w2raw[:].rearrange("p (a c) -> p a c", a=4), in_=w2.rearrange("(a p) c -> p a c", p=P)
+        )
+        for i in range(8):
+            nc.sync.dma_start(out=hraw[i][:], in_=hf[P * i : P * i + P, :])
+        for g in range(PASSES):
+            nc.sync.dma_start(
+                out=wraw[g][:].rearrange("p (u x) -> p u x", u=2),
+                in_=wm[512 * g : 512 * g + 512, :].rearrange("(u q e) c -> q u (e c)", u=2, e=2),
+            )
+        make_identity(nc, ident_b[:])
+        make_identity(nc, ident_f[:])
+        nc.vector.memset(gb[:], 0.0)
+        nc.vector.memset(bz[:], 0.0)
+        nc.vector.memset(eps[:], EPS)
+        nc.vector.memset(ones[:], 1.0)
+        nc.scalar.dma_start(out=gb[0:4, :], in_=gamma.rearrange("(t p) -> t p", p=P))
+        nc.scalar.dma_start(out=gb[4:8, :], in_=beta.rearrange("(t p) -> t p", p=P))
+        nc.scalar.dma_start(out=bz[0:1, :], in_=b2.rearrange("(o c) -> o c", o=1))
+        nc.scalar.activation(out=warm[:], in_=eps[:], func=ACT.Sqrt)
+
+        def w2_prepare():
+            for ap in range(2):
+                xw = psum.tile([P, 1024], BF16, name="xw", tag="bank%d" % ap)
+                for a2 in range(2):
+                    for t in range(4):
+                        a = 2 * ap + a2
+                        k = 4 * a2 + t
+                        nc.tensor.transpose(
+                            xw[:, P * k : P * k + P],
+                            w2raw[:, C * a + P * t : C * a + P * t + P],
+                            ident_b[:],
+                        )
+                nc.scalar.copy(
+                    out=w2g[:, 1024 * ap : 1024 * ap + 1024].rearrange("p (a o t) -> p a o t", a=2, t=4),
+                    in_=xw[:].rearrange("p (a t o) -> p a o t", a=2, t=4),
+                )
+
+        G = {}
+
+        def transpose_tile(i, vector_banks):
+            j, ii = divmod(i, 2)
+            words = hraw[i][:].bitcast(F32)
+            for gp in range(3):
+                if ii == 0:
+                    G[(j, gp)] = ring.tile([P, 2048], BF16, name="G%d" % gp, align_bytes=64)
+                xt = psum.tile([P, 512], F32, name="xt", tag="bank%d" % ((4 + 3 * i + gp) % 8))
+                for k in range(4):
+                    w0 = 512 * gp + P * k
+                    nc.tensor.transpose(xt[:, P * k : P * k + P], words[:, w0 : w0 + P], ident_f[:])
+                dst = G[(j, gp)][:].bitcast(F32).rearrange("p (g r u) -> p g r u", g=2, u=2)
+                dst = dst[:, :, P * ii : P * ii + P, :]
+                src = xt[:].rearrange("p (g u r) -> p g r u", g=2, u=2)
+                if gp in vector_banks:
+                    nc.vector.tensor_copy(out=dst, in_=src)
+                else:
+                    nc.scalar.copy(out=dst, in_=src)
+
+        def q_hops(j, g):
+            gp, g2 = divmod(g, 2)
+            c0 = g * ROWS + 256 * j
+            nc.vector.quantize_mx(
+                out=hc[:, c0 : c0 + 256].bitcast(FP8X4),
+                scales=hs[:, c0 : c0 + 256],
+                in_=G[(j, gp)][:, 1024 * g2 : 1024 * g2 + 1024],
+            )
+
+        def regroup(eng_copy, dst_flat, src_planes):
+            eng_copy(
+                out=dst_flat.rearrange("p (c i t) -> p c t i", i=4, t=4),
+                in_=src_planes.rearrange("p t (c i) -> p c t i", i=4),
+            )
+
+        def r_w(eng_copy, g, a):
+            regroup(
+                eng_copy,
+                wg[g][:, 1024 * a : 1024 * a + 1024],
+                wraw[g][:].rearrange("p (t x) -> p t x", t=4)[:, :, 256 * a : 256 * a + 256],
+            )
+
+        def q_w(g, a):
+            c0 = g * C + 256 * a
+            nc.vector.quantize_mx(
+                out=wc[:, c0 : c0 + 256].bitcast(FP8X4),
+                scales=ws[:, c0 : c0 + 256],
+                in_=wg[g][:, 1024 * a : 1024 * a + 1024],
+            )
+
+        z = {}
+        Z_BANK = {(0, 0): 4, (1, 0): 5, (0, 1): 6, (1, 1): 7, (2, 0): 0, (3, 0): 1, (2, 1): 2, (3, 1): 3}
+
+        def mx1(t, h, g):
+            if g == 0:
+                z[(t, h)] = psum.tile([P, 512], F32, name="z%d%d" % (t, h), tag="bank%d" % Z_BANK[(t, h)])
+            nc.tensor.matmul_mx(
+                out=z[(t, h)][:],
+                lhsT=wc[:, g * C + P * t : g * C + P * t + P].bitcast(FP8X4),
+                lhsT_scale=ws[:, g * C + P * t : g * C + P * t + P],
+                rhs=hc[:, g * ROWS + 512 * h : g * ROWS + 512 * h + 512].bitcast(FP8X4),
+                rhs_scale=hs[:, g * ROWS + 512 * h : g * ROWS + 512 * h + 512],
+                start=(g == 0),
+                stop=(g == PASSES - 1),
+            )
+
+        stats = [keep.tile([P, 12], F32, name="stats%d" % t) for t in range(4)]
+        mv = [keep.tile([P, 2], F32, name="mv%d" % t) for t in range(4)]
+        std = [keep.tile([P, 1], F32, name="std%d" % t) for t in range(4)]
+        nmean = [keep.tile([P, 1], F32, name="nmean%d" % t) for t in range(4)]
+        rstd = [keep.tile([P, 1], F32, name="rstd%d" % t) for t in range(4)]
+        scl = [keep.tile([P, 1], F32, name="scl%d" % t) for t in range(4)]
+        bia = [keep.tile([P, 1], F32, name="bia%d" % t) for t in range(4)]
+
+        def bn_stat(t, h):
+            nc.vector.bn_stats(out=stats[t][:, 6 * h : 6 * h + 6], in_=z[(t, h)][:])
+
+        def bn_chain(t):
+            nc.vector.bn_aggr(out=mv[t][:], in_=stats[t][:])
+            nc.scalar.activation(out=std[t][:], in_=mv[t][:, 1:2], func=ACT.Sqrt, bias=eps[:], scale=1.0)
+            nc.vector.tensor_scalar(out=nmean[t][:], in0=mv[t][:, 0:1], scalar1=-1.0, scalar2=None, op0=ALU.mult)
+            nc.vector.reciprocal(out=rstd[t][:], in_=std[t][:])
+            nc.vector.tensor_scalar(
+                out=scl[t][:], in0=rstd[t][:], scalar1=gbf[:, t : t + 1], scalar2=None, op0=ALU.mult
+            )
+            nc.vector.tensor_scalar(
+                out=bia[t][:],
+                in0=nmean[t][:],
+                scalar1=scl[t][:],
+                scalar2=gbf[:, 4 + t : 5 + t],
+                op0=ALU.mult,
+                op1=ALU.add,
+            )
+
+        def norm(t, r0, n):
+            h, c0 = divmod(r0, 512)
+            nc.scalar.activation(
+                out=yp[:, ROWS * t + r0 : ROWS * t + r0 + n],
+                in_=z[(t, h)][:, c0 : c0 + n],
+                func=ACT.Relu,
+                bias=bia[t][:],
+                scale=scl[t][:],
+            )
+
+        def r_y(eng_copy, rc):
+            regroup(
+                eng_copy,
+                yg[:, 1024 * rc : 1024 * rc + 1024],
+                yp[:].rearrange("p (t x) -> p t x", t=4)[:, :, 256 * rc : 256 * rc + 256],
+            )
+
+        def q_y(rc):
+            nc.vector.quantize_mx(
+                out=yc[:, 256 * rc : 256 * rc + 256].bitcast(FP8X4),
+                scales=ys[:, 256 * rc : 256 * rc + 256],
+                in_=yg[:, 1024 * rc : 1024 * rc + 1024],
+            )
+
+        O_BANK = [4, 5, 6, 7, 0, 2, 1, 3]
+        ops = {}
+
+        def mx2(i):
+            ops[i] = psum.tile([P, C], F32, name="ops", tag="bank%d" % O_BANK[i])
+            nc.tensor.matmul_mx(
+                out=ops[i][:],
+                lhsT=yc[:, P * i : P * i + P].bitcast(FP8X4),
+                lhsT_scale=ys[:, P * i : P * i + P],
+                rhs=w2c[:].bitcast(FP8X4),
+                rhs_scale=w2s[:],
+                start=True,
+                stop=True,
+            )
+
+        def finish(i):
+            ob = ring.tile([P, C], F32, name="ob", bufs=4)
+            nc.vector.tensor_tensor(out=ob[:], in0=ops[i][:], in1=b2bc[:], op=ALU.add)
+            nc.sync.dma_start(out=of[P * i : P * i + P, :], in_=ob[:])
+
+        vcopy = nc.vector.tensor_copy
+        scopy = nc.scalar.copy
+
+        w2_prepare()
+        nc.vector.quantize_mx(out=w2c[:].bitcast(FP8X4), scales=w2s[:], in_=w2g[:])
+        gps = psum.tile([P, P], BF16, name="gps", tag="bank2")
+        nc.tensor.transpose(gps[:], gb[:], ident_b[:])
+        nc.vector.tensor_copy(out=gbf[:], in_=gps[:, 0:8])
+        bps = psum.tile([P, C], F32, name="bps", tag="bank3")
+        nc.tensor.matmul(bps[:], lhsT=ones[:], rhs=bz[:], start=True, stop=True)
+        nc.vector.tensor_copy(out=b2bc[:], in_=bps[:])
+        for i in range(8):
+            transpose_tile(i, (2,) if i in (1, 3, 5) else ())
+            if i in (1, 3, 5):
+                for g in range(PASSES):
+                    q_hops(i // 2, g)
+
+        for g, a in ((1, 1), (2, 1), (3, 1), (4, 0), (5, 0), (4, 1), (5, 1)):
+            r_w(scopy, g, a)
+        q_hops(3, 0)
+        r_w(vcopy, 0, 0)
+        q_w(0, 0)
+        r_w(vcopy, 0, 1)
+        q_w(0, 1)
+        q_hops(3, 1)
+        r_w(vcopy, 1, 0)
+        q_w(1, 0)
+        q_w(1, 1)
+        q_hops(3, 2)
+        q_hops(3, 3)
+        r_w(vcopy, 2, 0)
+        q_w(2, 0)
+        q_hops(3, 4)
+        r_w(vcopy, 3, 0)
+        q_w(3, 0)
+        q_hops(3, 5)
+        q_w(4, 0)
+        q_w(5, 0)
+        for g in range(2, PASSES):
+            q_w(g, 1)
+
+        for g in range(2):
+            for t0 in (0, 2):
+                for h in range(2):
+                    for t in (t0, t0 + 1):
+                        mx1(t, h, g)
+        for g in range(2, PASSES):
+            for h in range(2):
+                for t in range(2):
+                    mx1(t, h, g)
+        for h in range(2):
+            for t in range(2):
+                bn_stat(t, h)
+        bn_chain(0)
+        bn_chain(1)
+        for t in range(2):
+            norm(t, 0, 512)
+            norm(t, 512, 512)
+        for t in (2, 3):
+            for h in range(2):
+                for g in range(2, PASSES):
+                    mx1(t, h, g)
+                bn_stat(t, h)
+            bn_chain(t)
+            if t == 2:
+                norm(t, 0, 512)
+                norm(t, 512, 512)
+
+        norm(3, 0, 256)
+        r_y(vcopy, 0)
+        q_y(0)
+        norm(3, 256, 256)
+        r_y(vcopy, 1)
+        q_y(1)
+        norm(3, 512, 256)
+        norm(3, 768, 256)
+        r_y(scopy, 2)
+        r_y(scopy, 3)
+        mx2(0)
+        mx2(1)
+        finish(0)
+        finish(1)
+        mx2(2)
+        mx2(3)
+        q_y(2)
+        finish(2)
+        finish(3)
+        mx2(4)
+        mx2(5)
+        q_y(3)
+        finish(4)
+        finish(5)
+        mx2(6)
+        mx2(7)
+        finish(6)
+        finish(7)

@@ -57,16 +57,18 @@ def tile_ginconvfft_pb_kernel(tc, hops, weight, gamma, beta, w2, b2, out):
         b2bc = keep.tile([P, C], F32, name="b2bc")
         gbf = keep.tile([P, 8], F32, name="gbf")
 
-        nc.sync.dma_start(
-            out=w2raw[:].rearrange("p (a c) -> p a c", a=4), in_=w2.rearrange("(a p) c -> p a c", p=P)
-        )
-        for i in range(8):
+        for i in range(4):
             nc.sync.dma_start(out=hraw[i][:], in_=hf[P * i : P * i + P, :])
         for g in range(PASSES):
             nc.sync.dma_start(
                 out=wraw[g][:].rearrange("p (u x) -> p u x", u=2),
                 in_=wm[512 * g : 512 * g + 512, :].rearrange("(u q e) c -> q u (e c)", u=2, e=2),
             )
+        for i in range(4, 8):
+            nc.sync.dma_start(out=hraw[i][:], in_=hf[P * i : P * i + P, :])
+        nc.sync.dma_start(
+            out=w2raw[:].rearrange("p (a c) -> p a c", a=4), in_=w2.rearrange("(a p) c -> p a c", p=P)
+        )
         make_identity(nc, ident_b[:])
         make_identity(nc, ident_f[:])
         nc.vector.memset(gb[:], 0.0)
@@ -78,9 +80,16 @@ def tile_ginconvfft_pb_kernel(tc, hops, weight, gamma, beta, w2, b2, out):
         nc.scalar.dma_start(out=bz[0:1, :], in_=b2.rearrange("(o c) -> o c", o=1))
         nc.scalar.activation(out=warm[:], in_=eps[:], func=ACT.Sqrt)
 
+        ring_count = [0]
+
+        def ring_bank():
+            n = ring_count[0]
+            ring_count[0] = n + 1
+            return "bank%d" % (4 + n % 4)
+
         def w2_prepare():
             for ap in range(2):
-                xw = psum.tile([P, 1024], BF16, name="xw", tag="bank%d" % ap)
+                xw = psum.tile([P, 1024], BF16, name="xw", tag=ring_bank())
                 for a2 in range(2):
                     for t in range(4):
                         a = 2 * ap + a2
@@ -103,7 +112,7 @@ def tile_ginconvfft_pb_kernel(tc, hops, weight, gamma, beta, w2, b2, out):
             for gp in range(3):
                 if ii == 0:
                     G[(j, gp)] = ring.tile([P, 2048], BF16, name="G%d" % gp, align_bytes=64)
-                xt = psum.tile([P, 512], F32, name="xt", tag="bank%d" % ((4 + 3 * i + gp) % 8))
+                xt = psum.tile([P, 512], F32, name="xt", tag=ring_bank())
                 for k in range(4):
                     w0 = 512 * gp + P * k
                     nc.tensor.transpose(xt[:, P * k : P * k + P], words[:, w0 : w0 + P], ident_f[:])
@@ -137,20 +146,16 @@ def tile_ginconvfft_pb_kernel(tc, hops, weight, gamma, beta, w2, b2, out):
                 wraw[g][:].rearrange("p (t x) -> p t x", t=4)[:, :, 256 * a : 256 * a + 256],
             )
 
-        def q_w(g, a):
-            c0 = g * C + 256 * a
+        def q_w(g):
             nc.vector.quantize_mx(
-                out=wc[:, c0 : c0 + 256].bitcast(FP8X4),
-                scales=ws[:, c0 : c0 + 256],
-                in_=wg[g][:, 1024 * a : 1024 * a + 1024],
+                out=wc[:, g * C : g * C + C].bitcast(FP8X4), scales=ws[:, g * C : g * C + C], in_=wg[g][:]
             )
 
         z = {}
-        Z_BANK = {(0, 0): 4, (1, 0): 5, (0, 1): 6, (1, 1): 7, (2, 0): 0, (3, 0): 1, (2, 1): 2, (3, 1): 3}
 
         def mx1(t, h, g):
             if g == 0:
-                z[(t, h)] = psum.tile([P, 512], F32, name="z%d%d" % (t, h), tag="bank%d" % Z_BANK[(t, h)])
+                z[(t, h)] = psum.tile([P, 512], F32, name="z%d%d" % (t, h), tag="bank%d" % (4 * h + t))
             nc.tensor.matmul_mx(
                 out=z[(t, h)][:],
                 lhsT=wc[:, g * C + P * t : g * C + P * t + P].bitcast(FP8X4),
@@ -172,10 +177,12 @@ def tile_ginconvfft_pb_kernel(tc, hops, weight, gamma, beta, w2, b2, out):
         def bn_stat(t, h):
             nc.vector.bn_stats(out=stats[t][:, 6 * h : 6 * h + 6], in_=z[(t, h)][:])
 
-        def bn_chain(t):
+        def bn_head(t):
             nc.vector.bn_aggr(out=mv[t][:], in_=stats[t][:])
             nc.scalar.activation(out=std[t][:], in_=mv[t][:, 1:2], func=ACT.Sqrt, bias=eps[:], scale=1.0)
             nc.vector.tensor_scalar(out=nmean[t][:], in0=mv[t][:, 0:1], scalar1=-1.0, scalar2=None, op0=ALU.mult)
+
+        def bn_tail(t):
             nc.vector.reciprocal(out=rstd[t][:], in_=std[t][:])
             nc.vector.tensor_scalar(
                 out=scl[t][:], in0=rstd[t][:], scalar1=gbf[:, t : t + 1], scalar2=None, op0=ALU.mult
@@ -213,7 +220,7 @@ def tile_ginconvfft_pb_kernel(tc, hops, weight, gamma, beta, w2, b2, out):
                 in_=yg[:, 1024 * rc : 1024 * rc + 1024],
             )
 
-        O_BANK = [4, 5, 6, 7, 0, 2, 1, 3]
+        O_BANK = [0, 4, 1, 5, 2, 6, 3, 7]
         ops = {}
 
         def mx2(i):
@@ -236,70 +243,62 @@ def tile_ginconvfft_pb_kernel(tc, hops, weight, gamma, beta, w2, b2, out):
         vcopy = nc.vector.tensor_copy
         scopy = nc.scalar.copy
 
-        w2_prepare()
-        nc.vector.quantize_mx(out=w2c[:].bitcast(FP8X4), scales=w2s[:], in_=w2g[:])
-        gps = psum.tile([P, P], BF16, name="gps", tag="bank2")
-        nc.tensor.transpose(gps[:], gb[:], ident_b[:])
-        nc.vector.tensor_copy(out=gbf[:], in_=gps[:, 0:8])
-        bps = psum.tile([P, C], F32, name="bps", tag="bank3")
-        nc.tensor.matmul(bps[:], lhsT=ones[:], rhs=bz[:], start=True, stop=True)
-        nc.vector.tensor_copy(out=b2bc[:], in_=bps[:])
-        for i in range(8):
-            transpose_tile(i, (2,) if i in (1, 3, 5) else ())
-            if i in (1, 3, 5):
+        for i in range(4):
+            transpose_tile(i, ())
+            if i == 1:
                 for g in range(PASSES):
-                    q_hops(i // 2, g)
+                    q_hops(0, g)
 
-        for g, a in ((1, 1), (2, 1), (3, 1), (4, 0), (5, 0), (4, 1), (5, 1)):
-            r_w(scopy, g, a)
-        q_hops(3, 0)
+        for g in range(1, PASSES):
+            r_w(scopy, g, 1)
         r_w(vcopy, 0, 0)
-        q_w(0, 0)
         r_w(vcopy, 0, 1)
-        q_w(0, 1)
-        q_hops(3, 1)
-        r_w(vcopy, 1, 0)
-        q_w(1, 0)
-        q_w(1, 1)
-        q_hops(3, 2)
-        q_hops(3, 3)
-        r_w(vcopy, 2, 0)
-        q_w(2, 0)
-        q_hops(3, 4)
-        r_w(vcopy, 3, 0)
-        q_w(3, 0)
-        q_hops(3, 5)
-        q_w(4, 0)
-        q_w(5, 0)
-        for g in range(2, PASSES):
-            q_w(g, 1)
+        q_w(0)
+        q_hops(1, 0)
+        q_hops(1, 1)
+        for g in range(1, PASSES):
+            r_w(vcopy, g, 0)
+            q_w(g)
+            if g + 1 < PASSES:
+                q_hops(1, g + 1)
 
-        for g in range(2):
-            for t0 in (0, 2):
-                for h in range(2):
-                    for t in (t0, t0 + 1):
-                        mx1(t, h, g)
-        for g in range(2, PASSES):
-            for h in range(2):
-                for t in range(2):
-                    mx1(t, h, g)
-        for h in range(2):
-            for t in range(2):
-                bn_stat(t, h)
-        bn_chain(0)
-        bn_chain(1)
-        for t in range(2):
-            norm(t, 0, 512)
-            norm(t, 512, 512)
-        for t in (2, 3):
-            for h in range(2):
-                for g in range(2, PASSES):
-                    mx1(t, h, g)
-                bn_stat(t, h)
-            bn_chain(t)
+        for g in range(PASSES):
+            for t in range(4):
+                mx1(t, 0, g)
+            if g == 3:
+                transpose_tile(4, ())
+                gps = psum.tile([P, P], BF16, name="gps", tag=ring_bank())
+                nc.tensor.transpose(gps[:], gb[:], ident_b[:])
+                nc.vector.tensor_copy(out=gbf[:], in_=gps[:, 0:8])
+                bps = psum.tile([P, C], F32, name="bps", tag=ring_bank())
+                nc.tensor.matmul(bps[:], lhsT=ones[:], rhs=bz[:], start=True, stop=True)
+                nc.vector.tensor_copy(out=b2bc[:], in_=bps[:])
+            if g == 4:
+                transpose_tile(5, ())
+                for gg in range(PASSES):
+                    q_hops(2, gg)
+        bn_stat(0, 0)
+        bn_stat(1, 0)
+        transpose_tile(6, ())
+        transpose_tile(7, ())
+        for g in range(PASSES):
+            q_hops(3, g)
+        w2_prepare()
+
+        for t in range(4):
+            for g in range(PASSES):
+                mx1(t, 1, g)
+            bn_stat(t, 1)
+            bn_head(t)
+            if t > 0:
+                norm(t - 1, 512, 512)
+            if t < 2:
+                bn_stat(t + 2, 0)
             if t == 2:
+                nc.vector.quantize_mx(out=w2c[:].bitcast(FP8X4), scales=w2s[:], in_=w2g[:])
+            bn_tail(t)
+            if t < 3:
                 norm(t, 0, 512)
-                norm(t, 512, 512)
 
         norm(3, 0, 256)
         r_y(vcopy, 0)

@@ -17,6 +17,7 @@ K1 = 3072
 C = 512
 PASSES = K1 // 512
 EPS = 1e-5
+SG_TILES = 3
 FLOPS = 2 * ROWS * K1 * C + 2 * ROWS * C * C
 
 
@@ -206,6 +207,20 @@ def tile_ginconvfft_pb_kernel(tc, hops, weight, gamma, beta, w2, b2, out):
                 scale=scl[t][:],
             )
 
+        def affine_on_vector(t, r0, n):
+            h, c0 = divmod(r0, 512)
+            nc.vector.tensor_scalar(
+                out=yp[:, ROWS * t + r0 : ROWS * t + r0 + n],
+                in0=z[(t, h)][:, c0 : c0 + n],
+                scalar1=scl[t][:],
+                scalar2=bia[t][:],
+                op0=ALU.mult,
+                op1=ALU.add,
+            )
+
+        def relu_copy(out, in_):
+            nc.vector.tensor_scalar(out=out, in0=in_, scalar1=0.0, scalar2=None, op0=ALU.max)
+
         def r_y(eng_copy, rc):
             regroup(
                 eng_copy,
@@ -235,10 +250,11 @@ def tile_ginconvfft_pb_kernel(tc, hops, weight, gamma, beta, w2, b2, out):
                 stop=True,
             )
 
+        ob = [keep.tile([P, C], F32, name="ob%d" % i) for i in range(8)]
+
         def finish(i):
-            ob = ring.tile([P, C], F32, name="ob", bufs=4)
-            nc.vector.tensor_tensor(out=ob[:], in0=ops[i][:], in1=b2bc[:], op=ALU.add)
-            nc.sync.dma_start(out=of[P * i : P * i + P, :], in_=ob[:])
+            nc.vector.tensor_tensor(out=ob[i][:], in0=ops[i][:], in1=b2bc[:], op=ALU.add)
+            nc.sync.dma_start(out=of[P * i : P * i + P, :], in_=ob[i][:])
 
         vcopy = nc.vector.tensor_copy
         scopy = nc.scalar.copy
@@ -253,14 +269,11 @@ def tile_ginconvfft_pb_kernel(tc, hops, weight, gamma, beta, w2, b2, out):
             r_w(scopy, g, 1)
         r_w(vcopy, 0, 0)
         r_w(vcopy, 0, 1)
-        q_w(0)
-        q_hops(1, 0)
-        q_hops(1, 1)
-        for g in range(1, PASSES):
-            r_w(vcopy, g, 0)
-            q_w(g)
+        for g in range(PASSES):
             if g + 1 < PASSES:
-                q_hops(1, g + 1)
+                r_w(vcopy, g + 1, 0)
+            q_w(g)
+            q_hops(1, g)
 
         for g in range(PASSES):
             for t in range(4):
@@ -300,31 +313,21 @@ def tile_ginconvfft_pb_kernel(tc, hops, weight, gamma, beta, w2, b2, out):
             if t < 3:
                 norm(t, 0, 512)
 
-        norm(3, 0, 256)
-        r_y(vcopy, 0)
-        q_y(0)
-        norm(3, 256, 256)
-        r_y(vcopy, 1)
-        q_y(1)
-        norm(3, 512, 256)
-        norm(3, 768, 256)
-        r_y(scopy, 2)
+        affine_on_vector(3, 0, 256)
+        r_y(relu_copy, 0)
+        for rc in range(1, 4):
+            norm(3, 256 * rc, 256)
         r_y(scopy, 3)
-        mx2(0)
-        mx2(1)
-        finish(0)
-        finish(1)
-        mx2(2)
-        mx2(3)
-        q_y(2)
-        finish(2)
-        finish(3)
-        mx2(4)
-        mx2(5)
-        q_y(3)
-        finish(4)
-        finish(5)
-        mx2(6)
-        mx2(7)
-        finish(6)
-        finish(7)
+        for rc in range(4):
+            if rc + 1 < 3:
+                r_y(vcopy, rc + 1)
+            q_y(rc)
+        for i in range(8):
+            mx2(i)
+        for i in range(SG_TILES):
+            nc.scalar.copy(out=ob[i][:], in_=ops[i][:])
+            nc.gpsimd.tensor_tensor(out=ob[i][:], in0=ob[i][:], in1=b2bc[:], op=ALU.add)
+        for i in range(SG_TILES):
+            nc.scalar.dma_start(out=of[P * i : P * i + P, :], in_=ob[i][:])
+        for i in range(SG_TILES, 8):
+            finish(i)

@@ -17,7 +17,6 @@ K1 = 3072
 C = 512
 PASSES = K1 // 512
 EPS = 1e-5
-SG_TILES = 3
 FLOPS = 2 * ROWS * K1 * C + 2 * ROWS * C * C
 
 
@@ -58,6 +57,9 @@ def tile_ginconvfft_pb_kernel(tc, hops, weight, gamma, beta, w2, b2, out):
         b2bc = keep.tile([P, C], F32, name="b2bc")
         gbf = keep.tile([P, 8], F32, name="gbf")
 
+        nc.sync.dma_start(
+            out=w2raw[:].rearrange("p (a c) -> p a c", a=4), in_=w2.rearrange("(a p) c -> p a c", p=P)
+        )
         for i in range(4):
             nc.sync.dma_start(out=hraw[i][:], in_=hf[P * i : P * i + P, :])
         for g in range(PASSES):
@@ -67,9 +69,6 @@ def tile_ginconvfft_pb_kernel(tc, hops, weight, gamma, beta, w2, b2, out):
             )
         for i in range(4, 8):
             nc.sync.dma_start(out=hraw[i][:], in_=hf[P * i : P * i + P, :])
-        nc.sync.dma_start(
-            out=w2raw[:].rearrange("p (a c) -> p a c", a=4), in_=w2.rearrange("(a p) c -> p a c", p=P)
-        )
         make_identity(nc, ident_b[:])
         make_identity(nc, ident_f[:])
         nc.vector.memset(gb[:], 0.0)
@@ -100,7 +99,7 @@ def tile_ginconvfft_pb_kernel(tc, hops, weight, gamma, beta, w2, b2, out):
                             w2raw[:, C * a + P * t : C * a + P * t + P],
                             ident_b[:],
                         )
-                nc.scalar.copy(
+                nc.vector.tensor_copy(
                     out=w2g[:, 1024 * ap : 1024 * ap + 1024].rearrange("p (a o t) -> p a o t", a=2, t=4),
                     in_=xw[:].rearrange("p (a t o) -> p a o t", a=2, t=4),
                 )
@@ -259,6 +258,8 @@ def tile_ginconvfft_pb_kernel(tc, hops, weight, gamma, beta, w2, b2, out):
         vcopy = nc.vector.tensor_copy
         scopy = nc.scalar.copy
 
+        w2_prepare()
+        nc.vector.quantize_mx(out=w2c[:].bitcast(FP8X4), scales=w2s[:], in_=w2g[:])
         for i in range(4):
             transpose_tile(i, ())
             if i == 1:
@@ -290,13 +291,12 @@ def tile_ginconvfft_pb_kernel(tc, hops, weight, gamma, beta, w2, b2, out):
                 transpose_tile(5, ())
                 for gg in range(PASSES):
                     q_hops(2, gg)
-        bn_stat(0, 0)
-        bn_stat(1, 0)
+        for t in range(4):
+            bn_stat(t, 0)
         transpose_tile(6, ())
         transpose_tile(7, ())
         for g in range(PASSES):
             q_hops(3, g)
-        w2_prepare()
 
         for t in range(4):
             for g in range(PASSES):
@@ -304,30 +304,21 @@ def tile_ginconvfft_pb_kernel(tc, hops, weight, gamma, beta, w2, b2, out):
             bn_stat(t, 1)
             bn_head(t)
             if t > 0:
+                bn_tail(t - 1)
+                norm(t - 1, 0, 512)
                 norm(t - 1, 512, 512)
-            if t < 2:
-                bn_stat(t + 2, 0)
-            if t == 2:
-                nc.vector.quantize_mx(out=w2c[:].bitcast(FP8X4), scales=w2s[:], in_=w2g[:])
-            bn_tail(t)
-            if t < 3:
-                norm(t, 0, 512)
+        bn_tail(3)
 
         affine_on_vector(3, 0, 256)
         r_y(relu_copy, 0)
+        q_y(0)
         for rc in range(1, 4):
             norm(3, 256 * rc, 256)
-        r_y(scopy, 3)
-        for rc in range(4):
-            if rc + 1 < 3:
-                r_y(vcopy, rc + 1)
+        r_y(vcopy, 1)
+        q_y(1)
+        for rc in (2, 3):
+            r_y(scopy, rc)
             q_y(rc)
         for i in range(8):
             mx2(i)
-        for i in range(SG_TILES):
-            nc.scalar.copy(out=ob[i][:], in_=ops[i][:])
-            nc.gpsimd.tensor_tensor(out=ob[i][:], in0=ob[i][:], in1=b2bc[:], op=ALU.add)
-        for i in range(SG_TILES):
-            nc.scalar.dma_start(out=of[P * i : P * i + P, :], in_=ob[i][:])
-        for i in range(SG_TILES, 8):
             finish(i)

@@ -17,6 +17,7 @@ K1 = 3072
 C = 512
 PASSES = K1 // 512
 EPS = 1e-5
+EARLY_W = (4,)
 FLOPS = 2 * ROWS * K1 * C + 2 * ROWS * C * C
 
 
@@ -57,18 +58,26 @@ def tile_ginconvfft_pb_kernel(tc, hops, weight, gamma, beta, w2, b2, out):
         b2bc = keep.tile([P, C], F32, name="b2bc")
         gbf = keep.tile([P, 8], F32, name="gbf")
 
-        nc.sync.dma_start(
-            out=w2raw[:].rearrange("p (a c) -> p a c", a=4), in_=w2.rearrange("(a p) c -> p a c", p=P)
-        )
-        for i in range(4):
-            nc.sync.dma_start(out=hraw[i][:], in_=hf[P * i : P * i + P, :])
-        for g in range(PASSES):
+        for a in range(4):
+            nc.sync.dma_start(out=w2raw[:, C * a : C * a + C], in_=w2[P * a : P * a + P, :])
+        def load_weights(g):
             nc.sync.dma_start(
                 out=wraw[g][:].rearrange("p (u x) -> p u x", u=2),
                 in_=wm[512 * g : 512 * g + 512, :].rearrange("(u q e) c -> q u (e c)", u=2, e=2),
             )
-        for i in range(4, 8):
-            nc.sync.dma_start(out=hraw[i][:], in_=hf[P * i : P * i + P, :])
+
+        for i in range(8):
+            if i in EARLY_W:
+                load_weights(EARLY_W.index(i))
+            pieces = 3 if i == 0 else 1
+            width = K1 // pieces
+            for s in range(pieces):
+                nc.sync.dma_start(
+                    out=hraw[i][:, width * s : width * s + width],
+                    in_=hf[P * i : P * i + P, width * s : width * s + width],
+                )
+        for g in range(len(EARLY_W), PASSES):
+            load_weights(g)
         make_identity(nc, ident_b[:])
         make_identity(nc, ident_f[:])
         nc.vector.memset(gb[:], 0.0)
@@ -260,43 +269,39 @@ def tile_ginconvfft_pb_kernel(tc, hops, weight, gamma, beta, w2, b2, out):
 
         w2_prepare()
         nc.vector.quantize_mx(out=w2c[:].bitcast(FP8X4), scales=w2s[:], in_=w2g[:])
-        for i in range(4):
+        for i in range(8):
             transpose_tile(i, ())
-            if i == 1:
-                for g in range(PASSES):
-                    q_hops(0, g)
-
-        for g in range(1, PASSES):
-            r_w(scopy, g, 1)
-        r_w(vcopy, 0, 0)
-        r_w(vcopy, 0, 1)
-        for g in range(PASSES):
-            if g + 1 < PASSES:
-                r_w(vcopy, g + 1, 0)
-            q_w(g)
-            q_hops(1, g)
-
-        for g in range(PASSES):
-            for t in range(4):
-                mx1(t, 0, g)
-            if g == 3:
-                transpose_tile(4, ())
+            if i == 2:
                 gps = psum.tile([P, P], BF16, name="gps", tag=ring_bank())
                 nc.tensor.transpose(gps[:], gb[:], ident_b[:])
                 nc.vector.tensor_copy(out=gbf[:], in_=gps[:, 0:8])
                 bps = psum.tile([P, C], F32, name="bps", tag=ring_bank())
                 nc.tensor.matmul(bps[:], lhsT=ones[:], rhs=bz[:], start=True, stop=True)
                 nc.vector.tensor_copy(out=b2bc[:], in_=bps[:])
-            if g == 4:
-                transpose_tile(5, ())
-                for gg in range(PASSES):
-                    q_hops(2, gg)
-        for t in range(4):
-            bn_stat(t, 0)
-        transpose_tile(6, ())
-        transpose_tile(7, ())
+            if i in (1, 3, 5):
+                for g in range(PASSES):
+                    q_hops(i // 2, g)
+            if i in (3, 5):
+                g = (i - 3) // 2
+                r_w(vcopy, g, 0)
+                r_w(vcopy, g, 1)
+                q_w(g)
+
+        for g in range(2, PASSES):
+            r_w(scopy, g, 1)
+        r_w(vcopy, 2, 0)
+        for g in range(2, PASSES):
+            if g + 1 < PASSES:
+                r_w(vcopy, g + 1, 0)
+            q_w(g)
         for g in range(PASSES):
             q_hops(3, g)
+
+        for g in range(PASSES):
+            for t in range(4):
+                mx1(t, 0, g)
+        for t in range(4):
+            bn_stat(t, 0)
 
         for t in range(4):
             for g in range(PASSES):
@@ -316,9 +321,15 @@ def tile_ginconvfft_pb_kernel(tc, hops, weight, gamma, beta, w2, b2, out):
             norm(3, 256 * rc, 256)
         r_y(vcopy, 1)
         q_y(1)
-        for rc in (2, 3):
-            r_y(scopy, rc)
-            q_y(rc)
-        for i in range(8):
-            mx2(i)
-            finish(i)
+        r_y(scopy, 2)
+        r_y(scopy, 3)
+        for rc in range(4):
+            if rc > 1:
+                q_y(rc)
+            for i in (2 * rc, 2 * rc + 1):
+                mx2(i)
+            if rc > 0:
+                finish(2 * rc - 2)
+                finish(2 * rc - 1)
+        finish(6)
+        finish(7)

@@ -155,16 +155,19 @@ def tile_ginconvfft_pb_kernel(tc, hops, weight, gamma, beta, w2, b2, out):
                 wraw[g][:].rearrange("p (t x) -> p t x", t=4)[:, :, 256 * a : 256 * a + 256],
             )
 
-        def q_w(g):
+        def q_w(g, a):
+            c0 = g * C + 256 * a
             nc.vector.quantize_mx(
-                out=wc[:, g * C : g * C + C].bitcast(FP8X4), scales=ws[:, g * C : g * C + C], in_=wg[g][:]
+                out=wc[:, c0 : c0 + 256].bitcast(FP8X4),
+                scales=ws[:, c0 : c0 + 256],
+                in_=wg[g][:, 1024 * a : 1024 * a + 1024],
             )
 
         z = {}
 
         def mx1(t, h, g):
             if g == 0:
-                z[(t, h)] = psum.tile([P, 512], F32, name="z%d%d" % (t, h), tag="bank%d" % (4 * h + t))
+                z[(t, h)] = psum.tile([P, 512], F32, name="z%d%d" % (t, h), tag="bank%d" % (2 * t + h))
             nc.tensor.matmul_mx(
                 out=z[(t, h)][:],
                 lhsT=wc[:, g * C + P * t : g * C + P * t + P].bitcast(FP8X4),
@@ -243,7 +246,7 @@ def tile_ginconvfft_pb_kernel(tc, hops, weight, gamma, beta, w2, b2, out):
                 in_=yg[:, 1024 * rc : 1024 * rc + 1024],
             )
 
-        O_BANK = [0, 4, 1, 5, 2, 6, 3, 7]
+        O_BANK = [0, 1, 2, 3, 4, 5, 6, 7]
         ops = {}
 
         def mx2(i):
@@ -281,50 +284,56 @@ def tile_ginconvfft_pb_kernel(tc, hops, weight, gamma, beta, w2, b2, out):
             if i in (1, 3, 5):
                 for g in range(PASSES):
                     q_hops(i // 2, g)
-            if i in (3, 5):
-                g = (i - 3) // 2
-                r_w(vcopy, g, 0)
-                r_w(vcopy, g, 1)
-                q_w(g)
+            if i == 3:
+                r_w(vcopy, 0, 0)
+                r_w(vcopy, 0, 1)
+                q_w(0, 0)
+                q_w(0, 1)
 
-        for g in range(2, PASSES):
+        for g in range(1, PASSES):
             r_w(scopy, g, 1)
-        r_w(vcopy, 2, 0)
-        for g in range(2, PASSES):
+        q_hops(3, 0)
+        r_w(vcopy, 1, 0)
+        for g in range(1, PASSES):
             if g + 1 < PASSES:
                 r_w(vcopy, g + 1, 0)
-            q_w(g)
-        for g in range(PASSES):
+            q_w(g, 0)
             q_hops(3, g)
+        for g in range(1, PASSES):
+            q_w(g, 1)
 
         for g in range(PASSES):
-            for t in range(4):
-                mx1(t, 0, g)
-        for t in range(4):
+            for h in range(2):
+                for t in range(2):
+                    mx1(t, h, g)
+        for t in range(2):
             bn_stat(t, 0)
-
-        for t in range(4):
-            for g in range(PASSES):
-                mx1(t, 1, g)
             bn_stat(t, 1)
             bn_head(t)
-            if t > 0:
-                bn_tail(t - 1)
-                norm(t - 1, 0, 512)
-                norm(t - 1, 512, 512)
-        bn_tail(3)
+        for t in range(2):
+            bn_tail(t)
+            norm(t, 0, 512)
+            norm(t, 512, 512)
+        for t in (2, 3):
+            for h in range(2):
+                for g in range(PASSES):
+                    mx1(t, h, g)
+                bn_stat(t, h)
+            bn_head(t)
+            bn_tail(t)
+            if t == 2:
+                norm(t, 0, 512)
+                norm(t, 512, 512)
 
         affine_on_vector(3, 0, 256)
         r_y(relu_copy, 0)
         q_y(0)
         for rc in range(1, 4):
             norm(3, 256 * rc, 256)
-        r_y(vcopy, 1)
-        q_y(1)
-        r_y(scopy, 2)
-        r_y(scopy, 3)
+        for rc in range(1, 4):
+            r_y(vcopy if rc < 2 else scopy, rc)
         for rc in range(4):
-            if rc > 1:
+            if rc > 0:
                 q_y(rc)
             for i in (2 * rc, 2 * rc + 1):
                 mx2(i)
@@ -332,4 +341,7 @@ def tile_ginconvfft_pb_kernel(tc, hops, weight, gamma, beta, w2, b2, out):
                 finish(2 * rc - 2)
                 finish(2 * rc - 1)
         finish(6)
-        finish(7)
+        for s in range(2):
+            cols = slice(256 * s, 256 * s + 256)
+            nc.vector.tensor_tensor(out=ob[7][:, cols], in0=ops[7][:, cols], in1=b2bc[:, cols], op=ALU.add)
+            nc.sync.dma_start(out=of[P * 7 : P * 8, cols], in_=ob[7][:, cols])

from contextlib import ExitStack

import concourse.mybir as mybir
from concourse.masks import make_identity

F32 = mybir.dt.float32
BF16 = mybir.dt.bfloat16
U32 = mybir.dt.uint32
U8 = mybir.dt.uint8
FP8X4 = mybir.dt.float8_e4m3fn_x4
ACT = mybir.ActivationFunctionType
ALU = mybir.AluOpType

P = 128
ROWS = 1024
K1 = 3072
C = 512
PASSES = K1 // 512
EPS = 1e-5
EARLY_W = (4,)
FLOPS = 2 * ROWS * K1 * C + 2 * ROWS * C * C


def tile_ginconvfft_pb_kernel(tc, hops, weight, gamma, beta, w2, b2, out):
    nc = tc.nc
    hf = hops.rearrange("b n l m -> (b n) (l m)")
    wm = weight.rearrange("l m c -> (l m) c")
    of = out.rearrange("b n c -> (b n) c")

    with ExitStack() as ctx:
        keep = ctx.enter_context(tc.tile_pool(name="keep", bufs=1))
        ring = ctx.enter_context(tc.tile_pool(name="ring", bufs=2))
        psum = ctx.enter_context(tc.psum_pool(name="psum", bufs=1))
        ctx.enter_context(tc.manual_schedule())

        eps = keep.tile([P, 1], F32, name="eps")
        warm = keep.tile([P, 1], F32, name="warm")
        ident_f = keep.tile([P, P], F32, name="ident_f")
        ident_b = keep.tile([P, P], BF16, name="ident_b")
        ones = keep.tile([P, P], BF16, name="ones")
        gb = keep.tile([P, P], BF16, name="gb")
        bz = keep.tile([P, C], BF16, name="bz")
        hraw = [keep.tile([P, K1], BF16, name="hraw%d" % i) for i in range(8)]
        w2raw = keep.tile([P, 4 * C], BF16, name="w2raw")
        wraw = [keep.tile([P, 4 * C], BF16, name="wraw%d" % g) for g in range(PASSES)]
        wg = [keep.tile([P, 4 * C], BF16, name="wg%d" % g, align_bytes=64) for g in range(PASSES)]
        hc = keep.tile([P, PASSES * ROWS], U32, name="hc", align_bytes=64)
        hs = keep.tile([P, PASSES * ROWS], U8, name="hs", align_bytes=64)
        wc = keep.tile([P, PASSES * C], U32, name="wc", align_bytes=64)
        ws = keep.tile([P, PASSES * C], U8, name="ws", align_bytes=64)
        w2g = keep.tile([P, 4 * C], BF16, name="w2g", align_bytes=64)
        w2c = keep.tile([P, C], U32, name="w2c", align_bytes=64)
        w2s = keep.tile([P, C], U8, name="w2s", align_bytes=64)
        yp = keep.tile([P, 4 * ROWS], BF16, name="yp")
        yg = keep.tile([P, 4 * ROWS], BF16, name="yg", align_bytes=64)
        yc = keep.tile([P, ROWS], U32, name="yc", align_bytes=64)
        ys = keep.tile([P, ROWS], U8, name="ys", align_bytes=64)
        b2bc = keep.tile([P, C], F32, name="b2bc")
        gbf = keep.tile([P, 8], F32, name="gbf")

        for a in range(4):
            nc.sync.dma_start(out=w2raw[:, C * a : C * a + C], in_=w2[P * a : P * a + P, :])
        def load_weights(g):
            nc.sync.dma_start(
                out=wraw[g][:].rearrange("p (u x) -> p u x", u=2),
                in_=wm[512 * g : 512 * g + 512, :].rearrange("(u q e) c -> q u (e c)", u=2, e=2),
            )

        for i in range(8):
            if i in EARLY_W:
                load_weights(EARLY_W.index(i))
            pieces = 3 if i == 0 else 1
            width = K1 // pieces
            for s in range(pieces):
                nc.sync.dma_start(
                    out=hraw[i][:, width * s : width * s + width],
                    in_=hf[P * i : P * i + P, width * s : width * s + width],
                )
        for g in range(len(EARLY_W), PASSES):
            load_weights(g)
        make_identity(nc, ident_b[:])
        make_identity(nc, ident_f[:])
        nc.vector.memset(gb[:], 0.0)
        nc.vector.memset(bz[:], 0.0)
        nc.vector.memset(eps[:], EPS)
        nc.vector.memset(ones[:], 1.0)
        nc.scalar.dma_start(out=gb[0:4, :], in_=gamma.rearrange("(t p) -> t p", p=P))
        nc.scalar.dma_start(out=gb[4:8, :], in_=beta.rearrange("(t p) -> t p", p=P))
        nc.scalar.dma_start(out=bz[0:1, :], in_=b2.rearrange("(o c) -> o c", o=1))
        nc.scalar.activation(out=warm[:], in_=eps[:], func=ACT.Sqrt)

        ring_count = [0]

        def ring_bank():
            n = ring_count[0]
            ring_count[0] = n + 1
            return "bank%d" % (4 + n % 4)

        def w2_prepare():
            for ap in range(2):
                xw = psum.tile([P, 1024], BF16, name="xw", tag=ring_bank())
                for a2 in range(2):
                    for t in range(4):
                        a = 2 * ap + a2
                        k = 4 * a2 + t
                        nc.tensor.transpose(
                            xw[:, P * k : P * k + P],
                            w2raw[:, C * a + P * t : C * a + P * t + P],
                            ident_b[:],
                        )
                nc.vector.tensor_copy(
                    out=w2g[:, 1024 * ap : 1024 * ap + 1024].rearrange("p (a o t) -> p a o t", a=2, t=4),
                    in_=xw[:].rearrange("p (a t o) -> p a o t", a=2, t=4),
                )

        G = {}

        def transpose_tile(i, vector_banks):
            j, ii = divmod(i, 2)
            words = hraw[i][:].bitcast(F32)
            for gp in range(3):
                if ii == 0:
                    G[(j, gp)] = ring.tile([P, 2048], BF16, name="G%d" % gp, align_bytes=64)
                xt = psum.tile([P, 512], F32, name="xt", tag=ring_bank())
                for k in range(4):
                    w0 = 512 * gp + P * k
                    nc.tensor.transpose(xt[:, P * k : P * k + P], words[:, w0 : w0 + P], ident_f[:])
                dst = G[(j, gp)][:].bitcast(F32).rearrange("p (g r u) -> p g r u", g=2, u=2)
                dst = dst[:, :, P * ii : P * ii + P, :]
                src = xt[:].rearrange("p (g u r) -> p g r u", g=2, u=2)
                if gp in vector_banks:
                    nc.vector.tensor_copy(out=dst, in_=src)
                else:
                    nc.scalar.copy(out=dst, in_=src)

        def q_hops(j, g):
            gp, g2 = divmod(g, 2)
            c0 = g * ROWS + 256 * j
            nc.vector.quantize_mx(
                out=hc[:, c0 : c0 + 256].bitcast(FP8X4),
                scales=hs[:, c0 : c0 + 256],
                in_=G[(j, gp)][:, 1024 * g2 : 1024 * g2 + 1024],
            )

        def regroup(eng_copy, dst_flat, src_planes):
            eng_copy(
                out=dst_flat.rearrange("p (c i t) -> p c t i", i=4, t=4),
                in_=src_planes.rearrange("p t (c i) -> p c t i", i=4),
            )

        def r_w(eng_copy, g, a):
            regroup(
                eng_copy,
                wg[g][:, 1024 * a : 1024 * a + 1024],
                wraw[g][:].rearrange("p (t x) -> p t x", t=4)[:, :, 256 * a : 256 * a + 256],
            )

        def q_w(g, a):
            c0 = g * C + 256 * a
            nc.vector.quantize_mx(
                out=wc[:, c0 : c0 + 256].bitcast(FP8X4),
                scales=ws[:, c0 : c0 + 256],
                in_=wg[g][:, 1024 * a : 1024 * a + 1024],
            )

        z = {}

        def mx1(t, h, g):
            if g == 0:
                z[(t, h)] = psum.tile([P, 512], F32, name="z%d%d" % (t, h), tag="bank%d" % (2 * t + h))
            nc.tensor.matmul_mx(
                out=z[(t, h)][:],
                lhsT=wc[:, g * C + P * t : g * C + P * t + P].bitcast(FP8X4),
                lhsT_scale=ws[:, g * C + P * t : g * C + P * t + P],
                rhs=hc[:, g * ROWS + 512 * h : g * ROWS + 512 * h + 512].bitcast(FP8X4),
                rhs_scale=hs[:, g * ROWS + 512 * h : g * ROWS + 512 * h + 512],
                start=(g == 0),
                stop=(g == PASSES - 1),
            )

        stats = [keep.tile([P, 12], F32, name="stats%d" % t) for t in range(4)]
        mv = [keep.tile([P, 2], F32, name="mv%d" % t) for t in range(4)]
        std = [keep.tile([P, 1], F32, name="std%d" % t) for t in range(4)]
        nmean = [keep.tile([P, 1], F32, name="nmean%d" % t) for t in range(4)]
        rstd = [keep.tile([P, 1], F32, name="rstd%d" % t) for t in range(4)]
        scl = [keep.tile([P, 1], F32, name="scl%d" % t) for t in range(4)]
        bia = [keep.tile([P, 1], F32, name="bia%d" % t) for t in range(4)]

        def bn_stat(t, h):
            nc.vector.bn_stats(out=stats[t][:, 6 * h : 6 * h + 6], in_=z[(t, h)][:])

        def bn_head(t):
            nc.vector.bn_aggr(out=mv[t][:], in_=stats[t][:])
            nc.scalar.activation(out=std[t][:], in_=mv[t][:, 1:2], func=ACT.Sqrt, bias=eps[:], scale=1.0)
            nc.vector.tensor_scalar(out=nmean[t][:], in0=mv[t][:, 0:1], scalar1=-1.0, scalar2=None, op0=ALU.mult)

        def bn_tail(t):
            nc.vector.reciprocal(out=rstd[t][:], in_=std[t][:])
            nc.vector.tensor_scalar(
                out=scl[t][:], in0=rstd[t][:], scalar1=gbf[:, t : t + 1], scalar2=None, op0=ALU.mult
            )
            nc.vector.tensor_scalar(
                out=bia[t][:],
                in0=nmean[t][:],
                scalar1=scl[t][:],
                scalar2=gbf[:, 4 + t : 5 + t],
                op0=ALU.mult,
                op1=ALU.add,
            )

        def norm(t, r0, n):
            h, c0 = divmod(r0, 512)
            nc.scalar.activation(
                out=yp[:, ROWS * t + r0 : ROWS * t + r0 + n],
                in_=z[(t, h)][:, c0 : c0 + n],
                func=ACT.Relu,
                bias=bia[t][:],
                scale=scl[t][:],
            )

        def affine_on_vector(t, r0, n):
            h, c0 = divmod(r0, 512)
            nc.vector.tensor_scalar(
                out=yp[:, ROWS * t + r0 : ROWS * t + r0 + n],
                in0=z[(t, h)][:, c0 : c0 + n],
                scalar1=scl[t][:],
                scalar2=bia[t][:],
                op0=ALU.mult,
                op1=ALU.add,
            )

        def relu_copy(out, in_):
            nc.vector.tensor_scalar(out=out, in0=in_, scalar1=0.0, scalar2=None, op0=ALU.max)

        def r_y(eng_copy, rc):
            regroup(
                eng_copy,
                yg[:, 1024 * rc : 1024 * rc + 1024],
                yp[:].rearrange("p (t x) -> p t x", t=4)[:, :, 256 * rc : 256 * rc + 256],
            )

        def q_y(rc):
            nc.vector.quantize_mx(
                out=yc[:, 256 * rc : 256 * rc + 256].bitcast(FP8X4),
                scales=ys[:, 256 * rc : 256 * rc + 256],
                in_=yg[:, 1024 * rc : 1024 * rc + 1024],
            )

        O_BANK = [0, 1, 2, 3, 4, 5, 6, 7]
        ops = {}

        def mx2(i):
            ops[i] = psum.tile([P, C], F32, name="ops", tag="bank%d" % O_BANK[i])
            nc.tensor.matmul_mx(
                out=ops[i][:],
                lhsT=yc[:, P * i : P * i + P].bitcast(FP8X4),
                lhsT_scale=ys[:, P * i : P * i + P],
                rhs=w2c[:].bitcast(FP8X4),
                rhs_scale=w2s[:],
                start=True,
                stop=True,
            )

        ob = [keep.tile([P, C], F32, name="ob%d" % i) for i in range(8)]

        def finish(i):
            nc.vector.tensor_tensor(out=ob[i][:], in0=ops[i][:], in1=b2bc[:], op=ALU.add)
            nc.sync.dma_start(out=of[P * i : P * i + P, :], in_=ob[i][:])

        vcopy = nc.vector.tensor_copy
        scopy = nc.scalar.copy

        w2_prepare()
        nc.vector.quantize_mx(out=w2c[:].bitcast(FP8X4), scales=w2s[:], in_=w2g[:])
        for i in range(8):
            transpose_tile(i, ())
            if i == 2:
                gps = psum.tile([P, P], BF16, name="gps", tag=ring_bank())
                nc.tensor.transpose(gps[:], gb[:], ident_b[:])
                nc.vector.tensor_copy(out=gbf[:], in_=gps[:, 0:8])
                bps = psum.tile([P, C], F32, name="bps", tag=ring_bank())
                nc.tensor.matmul(bps[:], lhsT=ones[:], rhs=bz[:], start=True, stop=True)
                nc.vector.tensor_copy(out=b2bc[:], in_=bps[:])
            if i in (1, 3, 5):
                for g in range(PASSES):
                    q_hops(i // 2, g)
            if i == 3:
                r_w(vcopy, 0, 0)
                r_w(vcopy, 0, 1)
                q_w(0, 0)
                q_w(0, 1)

        for g in range(1, PASSES):
            r_w(scopy, g, 1)
        q_hops(3, 0)
        r_w(vcopy, 1, 0)
        for g in range(1, PASSES):
            if g + 1 < PASSES:
                r_w(vcopy, g + 1, 0)
            q_w(g, 0)
            q_hops(3, g)
        for g in range(1, PASSES):
            q_w(g, 1)

        for g in range(PASSES):
            for h in range(2):
                for t in range(2):
                    mx1(t, h, g)
        for t in range(2):
            bn_stat(t, 0)
            bn_stat(t, 1)
            bn_head(t)
        for t in range(2):
            bn_tail(t)
            norm(t, 0, 512)
            norm(t, 512, 512)
        for t in (2, 3):
            for h in range(2):
                for g in range(PASSES):
                    mx1(t, h, g)
                bn_stat(t, h)
            bn_head(t)
            bn_tail(t)
            if t == 2:
                norm(t, 0, 512)
                norm(t, 512, 512)

        affine_on_vector(3, 0, 256)
        r_y(relu_copy, 0)
        q_y(0)
        for rc in range(1, 4):
            norm(3, 256 * rc, 256)
        for rc in range(1, 4):
            r_y(vcopy if rc < 2 else scopy, rc)
        for rc in range(4):
            if rc > 0:
                q_y(rc)
            for i in (2 * rc, 2 * rc + 1):
                mx2(i)
            if rc > 0:
                finish(2 * rc - 2)
                finish(2 * rc - 1)
        finish(6)
        for s in range(2):
            cols = slice(256 * s, 256 * s + 256)
            nc.vector.tensor_tensor(out=ob[7][:, cols], in0=ops[7][:, cols], in1=b2bc[:, cols], op=ALU.add)
            nc.sync.dma_start(out=of[P * 7 : P * 8, cols], in_=ob[7][:, cols])
